import numpy as np
import ml_dtypes


def mxq(x, axis, fmt="e4m3"):
    dtype, down = {"e4m3": (ml_dtypes.float8_e4m3fn, 7), "e5m2": (ml_dtypes.float8_e5m2, 14)}[fmt]
    v = np.moveaxis(np.asarray(x, np.float32).astype(ml_dtypes.bfloat16).astype(np.float64), axis, -1)
    blocks = v.reshape(v.shape[:-1] + (-1, 32))
    amax = np.abs(blocks).max(-1, keepdims=True)
    byte = np.maximum(np.where(amax > 0, np.frexp(amax)[1] - 1 + 127, 0) - down, 1)
    scale = np.exp2(byte - 127.0)
    codes = (blocks / scale).astype(np.float32).astype(dtype).astype(np.float64)
    return np.moveaxis((codes * scale).reshape(v.shape), -1, axis)


WIDE = False


def mx_kscale(k):
    if not WIDE:
        return np.ones(k)
    levels = np.array([10, -10, 5, -5, 0])
    a = np.random.permutation(np.resize(levels, k // 512 * 4)).reshape(k // 512, 4)
    idx = np.arange(k)
    return np.exp2(a[idx // 512, idx % 128 // 32])


BF16 = ml_dtypes.bfloat16


def bf(x):
    return np.asarray(x, np.float32).astype(BF16)


def f64(x):
    return np.asarray(x).astype(np.float64)


B, L, D, CH, S, R, NL = 1, 384, 1024, 2, 8, 128, 4
EPS = 1e-6


def rmsnorm(v, w):
    return v / np.sqrt(np.mean(v * v, axis=-1, keepdims=True) + EPS) * w


def setup_inputs():
    n = np.random.standard_normal
    t = mx_kscale(CH * D)
    return {"y": bf(n((B, L, CH * D)) * 0.9 * t),
            "x": bf(n((B, L, D))),
            "step_emb": bf(n(D) * 0.3),
            "out_proj_w": bf(n((D, CH * D)) / np.sqrt(CH * D) / t[None, :]),
            "mixer_norm_w": bf(1.0 + 0.1 * n(D)),
            "loop_norm_w": bf(1.0 + 0.1 * n(D))}


def reference(y, x, step_emb, out_proj_w, mixer_norm_w, loop_norm_w):
    h = f64(x) + f64(step_emb)
    out = rmsnorm(mxq(f64(y), 2, "e4m3") @ mxq(f64(out_proj_w), 1, "e4m3").T, f64(mixer_norm_w))
    return rmsnorm(h + out, f64(loop_norm_w))

@@ -1,0 +1,215 @@
+from contextlib import ExitStack
+
+import concourse.mybir as mybir
+from concourse.masks import make_identity
+
+F32 = mybir.dt.float32
+BF16 = mybir.dt.bfloat16
+I32 = mybir.dt.int32
+U32 = mybir.dt.uint32
+U8 = mybir.dt.uint8
+FP8X4 = mybir.dt.float8_e4m3fn_x4
+ACT = mybir.ActivationFunctionType
+ALU = mybir.AluOpType
+
+P = 128
+L, D, K = 384, 1024, 2048
+EPS = 1e-6
+PACK = 4
+PASSES = K // (P * PACK)
+BANK_PASSES = 2
+L_TILES = L // P
+CHUNK = 256
+CHUNK_TILES = CHUNK // P
+CHUNKS = D // CHUNK
+HALF = D // 2
+TILES_AHEAD = 1
+VECTOR_EVERY = 4
+
+FLOPS = 2 * L * D * K
+
+
+def tile_recursivemamba130m_pb_kernel(
+    tc, y, x, step_emb, out_proj_w, mixer_norm_w, loop_norm_w, out
+):
+    nc = tc.nc
+    y_rows = y.flatten_outer_dims()
+    x_rows = x.flatten_outer_dims()
+    out_rows = out.flatten_outer_dims()
+
+    with ExitStack() as ctx:
+        consts = ctx.enter_context(tc.tile_pool(name="consts", bufs=1))
+        raw = ctx.enter_context(tc.tile_pool(name="raw", bufs=1))
+        mx = ctx.enter_context(tc.tile_pool(name="mx", bufs=1))
+        stage = ctx.enter_context(tc.tile_pool(name="stage", bufs=2))
+        keep = ctx.enter_context(tc.tile_pool(name="keep", bufs=1))
+        work = ctx.enter_context(tc.tile_pool(name="work", bufs=2))
+        stats = ctx.enter_context(tc.tile_pool(name="stats", bufs=1))
+        tr_psum = ctx.enter_context(tc.psum_pool(name="tr_psum", bufs=5))
+        acc_psum = ctx.enter_context(tc.psum_pool(name="acc_psum", bufs=3))
+
+        vec_in = consts.tile([1, 3, D], BF16)
+        for i, vec in enumerate((mixer_norm_w, step_emb, loop_norm_w)):
+            nc.scalar.dma_start(out=vec_in[:, i, :], in_=vec.unsqueeze(0))
+
+        y_raw = [raw.tile([P, K], BF16, name="y_raw%d" % t) for t in range(L_TILES)]
+        x_raw = [raw.tile([P, D], BF16, name="x_raw%d" % t) for t in range(L_TILES)]
+        w_raw = [raw.tile([P, CHUNK_TILES, K], BF16, name="w_raw%d" % c) for c in range(CHUNKS)]
+
+        def load_y(t):
+            nc.sync.dma_start(out=y_raw[t][:], in_=y_rows[t * P : (t + 1) * P, :])
+
+        for t in range(TILES_AHEAD):
+            load_y(t)
+        for c in range(CHUNKS):
+            nc.sync.dma_start(
+                out=w_raw[c][:],
+                in_=out_proj_w[c * CHUNK : (c + 1) * CHUNK, :].rearrange("(i p) k -> p i k", p=P),
+            )
+        for t in range(L_TILES):
+            nc.sync.dma_start(out=x_raw[t][:], in_=x_rows[t * P : (t + 1) * P, :])
+            if t >= TILES_AHEAD:
+                load_y(t)
+
+        eps = consts.tile([P, 1], F32)
+        nc.vector.memset(eps[:], EPS)
+        warm = consts.tile([P, 1], F32)
+        nc.scalar.activation(out=warm[:], in_=eps[:], func=ACT.Sqrt)
+        ident = consts.tile([P, P], F32)
+        make_identity(nc, ident[:])
+        ones = consts.tile([P, P], BF16)
+        nc.vector.memset(ones[:], 1.0)
+
+        vec_rows = consts.tile([P, 3, D], BF16)
+        nc.vector.memset(vec_rows[:].bitcast(I32), 0)
+        nc.vector.tensor_copy(out=vec_rows[0:1, :, :], in_=vec_in[:])
+        spread = consts.tile([P, 3, D], BF16)
+        for i in range(3):
+            bank = tr_psum.tile([P, D], BF16, name="bank")
+            for n in range(2):
+                cols = slice(n * HALF, (n + 1) * HALF)
+                nc.tensor.matmul(
+                    out=bank[:, cols], lhsT=ones[:], rhs=vec_rows[:, i, cols], start=True, stop=True
+                )
+            nc.scalar.copy(out=spread[:, i, :], in_=bank[:])
+        mixer_gain = spread[:, 0, :]
+        step_row = spread[:, 1, :]
+        loop_gain = spread[:, 2, :]
+
+        def quantise_rows(row_tiles, staged, codes, scales, first_bank):
+            staged_words = staged[:].bitcast(F32)
+            for half in range(PASSES // BANK_PASSES):
+                passes = slice(half * BANK_PASSES, (half + 1) * BANK_PASSES)
+                for i, rows in enumerate(row_tiles):
+                    row_words = rows.bitcast(F32)
+                    bank = tr_psum.tile([P, BANK_PASSES, 2, P], F32, name="bank")
+                    for g in range(BANK_PASSES):
+                        for u in range(2):
+                            first = ((half * BANK_PASSES + g) * 2 + u) * P
+                            nc.tensor.transpose(
+                                bank[:, g, u, :], row_words[:, first : first + P], ident[:]
+                            )
+                    dst = staged_words[:, passes, i * P : (i + 1) * P, :]
+                    src = bank[:].rearrange("p g u r -> p g r u")
+                    bank_number = first_bank + half * len(row_tiles) + i
+                    if bank_number % VECTOR_EVERY == VECTOR_EVERY - 1:
+                        nc.vector.tensor_copy(out=dst, in_=src)
+                    else:
+                        nc.scalar.copy(out=dst, in_=src)
+                nc.vector.quantize_mx(
+                    out=codes[:, passes, :].rearrange("p g r -> p (g r)").bitcast(FP8X4),
+                    scales=scales[:, passes, :].rearrange("p g r -> p (g r)"),
+                    in_=staged[:, passes, :, :].rearrange("p g r t -> p (g r t)"),
+                )
+
+        y_codes = [mx.tile([P, PASSES, P], U32, name="y_codes%d" % t, align_bytes=64) for t in range(L_TILES)]
+        y_scales = [mx.tile([P, PASSES, P], U8, name="y_scales%d" % t, align_bytes=64) for t in range(L_TILES)]
+        w_codes = [mx.tile([P, PASSES, CHUNK], U32, name="w_codes%d" % c, align_bytes=64) for c in range(CHUNKS)]
+        w_scales = [mx.tile([P, PASSES, CHUNK], U8, name="w_scales%d" % c, align_bytes=64) for c in range(CHUNKS)]
+
+        def quantise_y(t):
+            y_staged = stage.tile([P, PASSES, P, PACK], BF16, align_bytes=64)
+            quantise_rows([y_raw[t][:]], y_staged, y_codes[t], y_scales[t], 2 * t)
+
+        def quantise_w(c):
+            w_staged = stage.tile([P, PASSES, CHUNK, PACK], BF16, align_bytes=64)
+            tiles = [w_raw[c][:, i, :] for i in range(CHUNK_TILES)]
+            quantise_rows(tiles, w_staged, w_codes[c], w_scales[c], 4 * c)
+
+        gained = [keep.tile([P, D], F32, name="gained%d" % t) for t in range(L_TILES)]
+        p_squares = [stats.tile([P, CHUNKS], F32, name="p_squares%d" % t) for t in range(L_TILES)]
+
+        def project(t, c):
+            acc = acc_psum.tile([P, CHUNK], F32)
+            for g in range(PASSES):
+                nc.tensor.matmul_mx(
+                    out=acc[:],
+                    lhsT=y_codes[t][:, g, :].bitcast(FP8X4),
+                    lhsT_scale=y_scales[t][:, g, :],
+                    rhs=w_codes[c][:, g, :].bitcast(FP8X4),
+                    rhs_scale=w_scales[c][:, g, :],
+                    start=(g == 0),
+                    stop=(g == PASSES - 1),
+                )
+            cols = slice(c * CHUNK, (c + 1) * CHUNK)
+            squares = work.tile([P, CHUNK], BF16, name="squares")
+            nc.scalar.activation(
+                out=squares[:], in_=acc[:], func=ACT.Square, accum_out=p_squares[t][:, c : c + 1]
+            )
+            nc.vector.tensor_tensor(
+                out=gained[t][:, cols], in0=acc[:], in1=mixer_gain[:, cols], op=ALU.mult
+            )
+
+        def inverse_rms(sum_of_squares, name):
+            rms = stats.tile([P, 1], F32, name="rms_" + name)
+            nc.scalar.activation(
+                out=rms[:], in_=sum_of_squares, func=ACT.Sqrt, scale=1.0 / D, bias=eps[:]
+            )
+            inverse = stats.tile([P, 1], F32, name="inv_" + name)
+            nc.vector.reciprocal(out=inverse[:], in_=rms[:])
+            return inverse
+
+        def residual(t):
+            h = keep.tile([P, D], F32, name="h%d" % t)
+            nc.gpsimd.tensor_tensor(out=h[:], in0=x_raw[t][:], in1=step_row, op=ALU.add)
+            return h
+
+        def finish(t, h):
+            scrap = stats.tile([P, CHUNKS], F32, name="scrap%d" % t)
+            p_square_sum = stats.tile([P, 1], F32, name="p_square_sum%d" % t)
+            nc.scalar.activation(
+                out=scrap[:], in_=p_squares[t][:], func=ACT.Copy, accum_out=p_square_sum[:]
+            )
+            inv_p = inverse_rms(p_square_sum[:], "p%d" % t)
+            v = work.tile([P, D], F32, name="v")
+            nc.vector.scalar_tensor_tensor(
+                out=v[:], in0=gained[t][:], scalar=inv_p[:], in1=h[:], op0=ALU.mult, op1=ALU.add
+            )
+            v_squares = work.tile([P, D], BF16, name="v_squares")
+            v_square_sum = stats.tile([P, 1], F32, name="v_square_sum%d" % t)
+            nc.scalar.activation(
+                out=v_squares[:], in_=v[:], func=ACT.Square, accum_out=v_square_sum[:]
+            )
+            inv_v = inverse_rms(v_square_sum[:], "v%d" % t)
+            result = work.tile([P, D], F32, name="result")
+            for n in range(2):
+                cols = slice(n * HALF, (n + 1) * HALF)
+                nc.vector.scalar_tensor_tensor(
+                    out=result[:, cols], in0=v[:, cols], scalar=inv_v[:], in1=loop_gain[:, cols],
+                    op0=ALU.mult, op1=ALU.mult,
+                )
+                nc.sync.dma_start(out=out_rows[t * P : (t + 1) * P, cols], in_=result[:, cols])
+
+        for t in range(TILES_AHEAD):
+            quantise_y(t)
+        for c in range(CHUNKS):
+            quantise_w(c)
+            for t in range(TILES_AHEAD):
+                project(t, c)
+        for t in range(TILES_AHEAD):
+            finish(t, residual(t))
+        for t in range(TILES_AHEAD, L_TILES):
+            quantise_y(t)
+            for c in range(CHUNKS):
+                project(t, c)
+            finish(t, residual(t))

@@ -18,12 +18,12 @@ EPS = 1e-6
 PACK = 4
 PASSES = K // (P * PACK)
 BANK_PASSES = 2
+TILE_BANKS = PASSES // BANK_PASSES
 L_TILES = L // P
 CHUNK = 256
 CHUNK_TILES = CHUNK // P
 CHUNKS = D // CHUNK
 HALF = D // 2
-TILES_AHEAD = 1
 VECTOR_EVERY = 4
 
 FLOPS = 2 * L * D * K
@@ -38,38 +38,32 @@ def tile_recursivemamba130m_pb_kernel(
     out_rows = out.flatten_outer_dims()
 
     with ExitStack() as ctx:
+        ctx.enter_context(tc.manual_schedule())
         consts = ctx.enter_context(tc.tile_pool(name="consts", bufs=1))
         raw = ctx.enter_context(tc.tile_pool(name="raw", bufs=1))
         mx = ctx.enter_context(tc.tile_pool(name="mx", bufs=1))
         stage = ctx.enter_context(tc.tile_pool(name="stage", bufs=2))
         keep = ctx.enter_context(tc.tile_pool(name="keep", bufs=1))
-        work = ctx.enter_context(tc.tile_pool(name="work", bufs=2))
+        scrap = ctx.enter_context(tc.tile_pool(name="scrap", bufs=2))
         stats = ctx.enter_context(tc.tile_pool(name="stats", bufs=1))
-        tr_psum = ctx.enter_context(tc.psum_pool(name="tr_psum", bufs=5))
-        acc_psum = ctx.enter_context(tc.psum_pool(name="acc_psum", bufs=3))
+        tr_psum = ctx.enter_context(tc.psum_pool(name="tr_psum", bufs=4))
+        acc_psum = ctx.enter_context(tc.psum_pool(name="acc_psum", bufs=4))
 
         vec_in = consts.tile([1, 3, D], BF16)
         for i, vec in enumerate((mixer_norm_w, step_emb, loop_norm_w)):
-            nc.scalar.dma_start(out=vec_in[:, i, :], in_=vec.unsqueeze(0))
-
+            nc.sync.dma_start(out=vec_in[:, i, :], in_=vec.unsqueeze(0))
         y_raw = [raw.tile([P, K], BF16, name="y_raw%d" % t) for t in range(L_TILES)]
-        x_raw = [raw.tile([P, D], BF16, name="x_raw%d" % t) for t in range(L_TILES)]
-        w_raw = [raw.tile([P, CHUNK_TILES, K], BF16, name="w_raw%d" % c) for c in range(CHUNKS)]
-
-        def load_y(t):
+        for t in range(L_TILES):
             nc.sync.dma_start(out=y_raw[t][:], in_=y_rows[t * P : (t + 1) * P, :])
-
-        for t in range(TILES_AHEAD):
-            load_y(t)
+        w_raw = [raw.tile([P, CHUNK_TILES, K], BF16, name="w_raw%d" % c) for c in range(CHUNKS)]
         for c in range(CHUNKS):
             nc.sync.dma_start(
                 out=w_raw[c][:],
                 in_=out_proj_w[c * CHUNK : (c + 1) * CHUNK, :].rearrange("(i p) k -> p i k", p=P),
             )
+        x_raw = [raw.tile([P, D], BF16, name="x_raw%d" % t) for t in range(L_TILES)]
         for t in range(L_TILES):
             nc.sync.dma_start(out=x_raw[t][:], in_=x_rows[t * P : (t + 1) * P, :])
-            if t >= TILES_AHEAD:
-                load_y(t)
 
         eps = consts.tile([P, 1], F32)
         nc.vector.memset(eps[:], EPS)
@@ -98,29 +92,28 @@ def tile_recursivemamba130m_pb_kernel(
 
         def quantise_rows(row_tiles, staged, codes, scales, first_bank):
             staged_words = staged[:].bitcast(F32)
-            for half in range(PASSES // BANK_PASSES):
-                passes = slice(half * BANK_PASSES, (half + 1) * BANK_PASSES)
-                for i, rows in enumerate(row_tiles):
-                    row_words = rows.bitcast(F32)
+            for i, rows in enumerate(row_tiles):
+                row_words = rows.bitcast(F32)
+                for b in range(TILE_BANKS):
                     bank = tr_psum.tile([P, BANK_PASSES, 2, P], F32, name="bank")
                     for g in range(BANK_PASSES):
                         for u in range(2):
-                            first = ((half * BANK_PASSES + g) * 2 + u) * P
+                            first = ((b * BANK_PASSES + g) * 2 + u) * P
                             nc.tensor.transpose(
                                 bank[:, g, u, :], row_words[:, first : first + P], ident[:]
                             )
+                    passes = slice(b * BANK_PASSES, (b + 1) * BANK_PASSES)
                     dst = staged_words[:, passes, i * P : (i + 1) * P, :]
                     src = bank[:].rearrange("p g u r -> p g r u")
-                    bank_number = first_bank + half * len(row_tiles) + i
-                    if bank_number % VECTOR_EVERY == VECTOR_EVERY - 1:
+                    if (first_bank + i * TILE_BANKS + b) % VECTOR_EVERY == 0:
                         nc.vector.tensor_copy(out=dst, in_=src)
                     else:
                         nc.scalar.copy(out=dst, in_=src)
-                nc.vector.quantize_mx(
-                    out=codes[:, passes, :].rearrange("p g r -> p (g r)").bitcast(FP8X4),
-                    scales=scales[:, passes, :].rearrange("p g r -> p (g r)"),
-                    in_=staged[:, passes, :, :].rearrange("p g r t -> p (g r t)"),
-                )
+            nc.vector.quantize_mx(
+                out=codes[:].rearrange("p g r -> p (g r)").bitcast(FP8X4),
+                scales=scales[:].rearrange("p g r -> p (g r)"),
+                in_=staged[:].rearrange("p g r t -> p (g r t)"),
+            )
 
         y_codes = [mx.tile([P, PASSES, P], U32, name="y_codes%d" % t, align_bytes=64) for t in range(L_TILES)]
         y_scales = [mx.tile([P, PASSES, P], U8, name="y_scales%d" % t, align_bytes=64) for t in range(L_TILES)]
@@ -129,12 +122,13 @@ def tile_recursivemamba130m_pb_kernel(
 
         def quantise_y(t):
             y_staged = stage.tile([P, PASSES, P, PACK], BF16, align_bytes=64)
-            quantise_rows([y_raw[t][:]], y_staged, y_codes[t], y_scales[t], 2 * t)
+            quantise_rows([y_raw[t][:]], y_staged, y_codes[t], y_scales[t], t * TILE_BANKS)
 
         def quantise_w(c):
             w_staged = stage.tile([P, PASSES, CHUNK, PACK], BF16, align_bytes=64)
             tiles = [w_raw[c][:, i, :] for i in range(CHUNK_TILES)]
-            quantise_rows(tiles, w_staged, w_codes[c], w_scales[c], 4 * c)
+            first_bank = (L_TILES + c * CHUNK_TILES) * TILE_BANKS
+            quantise_rows(tiles, w_staged, w_codes[c], w_scales[c], first_bank)
 
         gained = [keep.tile([P, D], F32, name="gained%d" % t) for t in range(L_TILES)]
         p_squares = [stats.tile([P, CHUNKS], F32, name="p_squares%d" % t) for t in range(L_TILES)]
@@ -152,7 +146,7 @@ def tile_recursivemamba130m_pb_kernel(
                     stop=(g == PASSES - 1),
                 )
             cols = slice(c * CHUNK, (c + 1) * CHUNK)
-            squares = work.tile([P, CHUNK], BF16, name="squares")
+            squares = scrap.tile([P, CHUNK], BF16, name="squares")
             nc.scalar.activation(
                 out=squares[:], in_=acc[:], func=ACT.Square, accum_out=p_squares[t][:, c : c + 1]
             )
@@ -160,56 +154,57 @@ def tile_recursivemamba130m_pb_kernel(
                 out=gained[t][:, cols], in0=acc[:], in1=mixer_gain[:, cols], op=ALU.mult
             )
 
-        def inverse_rms(sum_of_squares, name):
-            rms = stats.tile([P, 1], F32, name="rms_" + name)
+        def root_mean_square(sum_of_squares, name):
+            rms = stats.tile([P, 1], F32, name=name)
             nc.scalar.activation(
                 out=rms[:], in_=sum_of_squares, func=ACT.Sqrt, scale=1.0 / D, bias=eps[:]
             )
-            inverse = stats.tile([P, 1], F32, name="inv_" + name)
-            nc.vector.reciprocal(out=inverse[:], in_=rms[:])
-            return inverse
+            return rms
 
-        def residual(t):
-            h = keep.tile([P, D], F32, name="h%d" % t)
-            nc.gpsimd.tensor_tensor(out=h[:], in0=x_raw[t][:], in1=step_row, op=ALU.add)
-            return h
+        def inverse(rms, name):
+            inv = stats.tile([P, 1], F32, name=name)
+            nc.vector.reciprocal(out=inv[:], in_=rms[:])
+            return inv
 
-        def finish(t, h):
-            scrap = stats.tile([P, CHUNKS], F32, name="scrap%d" % t)
+        for t in range(L_TILES):
+            quantise_y(t)
+        quantise_w(0)
+
+        h = [keep.tile([P, D], F32, name="h%d" % t) for t in range(L_TILES)]
+        for t in range(L_TILES):
+            nc.gpsimd.tensor_tensor(out=h[t][:], in0=x_raw[t][:], in1=step_row, op=ALU.add)
+
+        for c in range(1, CHUNKS):
+            quantise_w(c)
+            for t in range(L_TILES):
+                project(t, c - 1)
+
+        v = [keep.tile([P, D], F32, name="v%d" % t) for t in range(L_TILES)]
+        for t in range(L_TILES):
+            project(t, CHUNKS - 1)
+            partial = stats.tile([P, CHUNKS], F32, name="partial%d" % t)
             p_square_sum = stats.tile([P, 1], F32, name="p_square_sum%d" % t)
             nc.scalar.activation(
-                out=scrap[:], in_=p_squares[t][:], func=ACT.Copy, accum_out=p_square_sum[:]
+                out=partial[:], in_=p_squares[t][:], func=ACT.Copy, accum_out=p_square_sum[:]
             )
-            inv_p = inverse_rms(p_square_sum[:], "p%d" % t)
-            v = work.tile([P, D], F32, name="v")
+            inv_p = inverse(root_mean_square(p_square_sum[:], "rms_p%d" % t), "inv_p%d" % t)
             nc.vector.scalar_tensor_tensor(
-                out=v[:], in0=gained[t][:], scalar=inv_p[:], in1=h[:], op0=ALU.mult, op1=ALU.add
+                out=v[t][:], in0=gained[t][:], scalar=inv_p[:], in1=h[t][:],
+                op0=ALU.mult, op1=ALU.add,
             )
-            v_squares = work.tile([P, D], BF16, name="v_squares")
+
+        for t in range(L_TILES):
+            v_squares = scrap.tile([P, D], BF16, name="v_squares")
             v_square_sum = stats.tile([P, 1], F32, name="v_square_sum%d" % t)
             nc.scalar.activation(
-                out=v_squares[:], in_=v[:], func=ACT.Square, accum_out=v_square_sum[:]
+                out=v_squares[:], in_=v[t][:], func=ACT.Square, accum_out=v_square_sum[:]
             )
-            inv_v = inverse_rms(v_square_sum[:], "v%d" % t)
-            result = work.tile([P, D], F32, name="result")
+            inv_v = inverse(root_mean_square(v_square_sum[:], "rms_v%d" % t), "inv_v%d" % t)
+            result = scrap.tile([P, D], F32, name="result")
             for n in range(2):
                 cols = slice(n * HALF, (n + 1) * HALF)
                 nc.vector.scalar_tensor_tensor(
-                    out=result[:, cols], in0=v[:, cols], scalar=inv_v[:], in1=loop_gain[:, cols],
+                    out=result[:, cols], in0=v[t][:, cols], scalar=inv_v[:], in1=loop_gain[:, cols],
                     op0=ALU.mult, op1=ALU.mult,
                 )
                 nc.sync.dma_start(out=out_rows[t * P : (t + 1) * P, cols], in_=result[:, cols])
-
-        for t in range(TILES_AHEAD):
-            quantise_y(t)
-        for c in range(CHUNKS):
-            quantise_w(c)
-            for t in range(TILES_AHEAD):
-                project(t, c)
-        for t in range(TILES_AHEAD):
-            finish(t, residual(t))
-        for t in range(TILES_AHEAD, L_TILES):
-            quantise_y(t)
-            for c in range(CHUNKS):
-                project(t, c)
-            finish(t, residual(t))

@@ -20,7 +20,7 @@ PASSES = K // (P * PACK)
 BANK_PASSES = 2
 TILE_BANKS = PASSES // BANK_PASSES
 L_TILES = L // P
-CHUNK = 256
+CHUNK = 128
 CHUNK_TILES = CHUNK // P
 CHUNKS = D // CHUNK
 HALF = D // 2

@@ -20,11 +20,12 @@ PASSES = K // (P * PACK)
 BANK_PASSES = 2
 TILE_BANKS = PASSES // BANK_PASSES
 L_TILES = L // P
-CHUNK = 128
+CHUNK = 256
 CHUNK_TILES = CHUNK // P
 CHUNKS = D // CHUNK
-HALF = D // 2
-VECTOR_EVERY = 4
+BANK = 512
+BANKS = D // BANK
+VECTOR_EVERY = 3
 
 FLOPS = 2 * L * D * K
 
@@ -52,15 +53,15 @@ def tile_recursivemamba130m_pb_kernel(
         vec_in = consts.tile([1, 3, D], BF16)
         for i, vec in enumerate((mixer_norm_w, step_emb, loop_norm_w)):
             nc.sync.dma_start(out=vec_in[:, i, :], in_=vec.unsqueeze(0))
-        y_raw = [raw.tile([P, K], BF16, name="y_raw%d" % t) for t in range(L_TILES)]
-        for t in range(L_TILES):
-            nc.sync.dma_start(out=y_raw[t][:], in_=y_rows[t * P : (t + 1) * P, :])
         w_raw = [raw.tile([P, CHUNK_TILES, K], BF16, name="w_raw%d" % c) for c in range(CHUNKS)]
         for c in range(CHUNKS):
             nc.sync.dma_start(
                 out=w_raw[c][:],
                 in_=out_proj_w[c * CHUNK : (c + 1) * CHUNK, :].rearrange("(i p) k -> p i k", p=P),
             )
+        y_raw = [raw.tile([P, K], BF16, name="y_raw%d" % t) for t in range(L_TILES)]
+        for t in range(L_TILES):
+            nc.sync.dma_start(out=y_raw[t][:], in_=y_rows[t * P : (t + 1) * P, :])
         x_raw = [raw.tile([P, D], BF16, name="x_raw%d" % t) for t in range(L_TILES)]
         for t in range(L_TILES):
             nc.sync.dma_start(out=x_raw[t][:], in_=x_rows[t * P : (t + 1) * P, :])
@@ -80,8 +81,8 @@ def tile_recursivemamba130m_pb_kernel(
         spread = consts.tile([P, 3, D], BF16)
         for i in range(3):
             bank = tr_psum.tile([P, D], BF16, name="bank")
-            for n in range(2):
-                cols = slice(n * HALF, (n + 1) * HALF)
+            for n in range(BANKS):
+                cols = slice(n * BANK, (n + 1) * BANK)
                 nc.tensor.matmul(
                     out=bank[:, cols], lhsT=ones[:], rhs=vec_rows[:, i, cols], start=True, stop=True
                 )
@@ -109,102 +110,109 @@ def tile_recursivemamba130m_pb_kernel(
                         nc.vector.tensor_copy(out=dst, in_=src)
                     else:
                         nc.scalar.copy(out=dst, in_=src)
-            nc.vector.quantize_mx(
-                out=codes[:].rearrange("p g r -> p (g r)").bitcast(FP8X4),
-                scales=scales[:].rearrange("p g r -> p (g r)"),
-                in_=staged[:].rearrange("p g r t -> p (g r t)"),
-            )
-
-        y_codes = [mx.tile([P, PASSES, P], U32, name="y_codes%d" % t, align_bytes=64) for t in range(L_TILES)]
-        y_scales = [mx.tile([P, PASSES, P], U8, name="y_scales%d" % t, align_bytes=64) for t in range(L_TILES)]
-        w_codes = [mx.tile([P, PASSES, CHUNK], U32, name="w_codes%d" % c, align_bytes=64) for c in range(CHUNKS)]
-        w_scales = [mx.tile([P, PASSES, CHUNK], U8, name="w_scales%d" % c, align_bytes=64) for c in range(CHUNKS)]
-
-        def quantise_y(t):
-            y_staged = stage.tile([P, PASSES, P, PACK], BF16, align_bytes=64)
-            quantise_rows([y_raw[t][:]], y_staged, y_codes[t], y_scales[t], t * TILE_BANKS)
-
-        def quantise_w(c):
-            w_staged = stage.tile([P, PASSES, CHUNK, PACK], BF16, align_bytes=64)
-            tiles = [w_raw[c][:, i, :] for i in range(CHUNK_TILES)]
-            first_bank = (L_TILES + c * CHUNK_TILES) * TILE_BANKS
-            quantise_rows(tiles, w_staged, w_codes[c], w_scales[c], first_bank)
-
-        gained = [keep.tile([P, D], F32, name="gained%d" % t) for t in range(L_TILES)]
-        p_squares = [stats.tile([P, CHUNKS], F32, name="p_squares%d" % t) for t in range(L_TILES)]
-
-        def project(t, c):
-            acc = acc_psum.tile([P, CHUNK], F32)
             for g in range(PASSES):
-                nc.tensor.matmul_mx(
-                    out=acc[:],
-                    lhsT=y_codes[t][:, g, :].bitcast(FP8X4),
-                    lhsT_scale=y_scales[t][:, g, :],
-                    rhs=w_codes[c][:, g, :].bitcast(FP8X4),
-                    rhs_scale=w_scales[c][:, g, :],
-                    start=(g == 0),
-                    stop=(g == PASSES - 1),
+                nc.vector.quantize_mx(
+                    out=codes[:, g, :].bitcast(FP8X4),
+                    scales=scales[:, g, :],
+                    in_=staged[:, g, :, :].rearrange("p r t -> p (r t)"),
                 )
-            cols = slice(c * CHUNK, (c + 1) * CHUNK)
-            squares = scrap.tile([P, CHUNK], BF16, name="squares")
-            nc.scalar.activation(
-                out=squares[:], in_=acc[:], func=ACT.Square, accum_out=p_squares[t][:, c : c + 1]
-            )
-            nc.vector.tensor_tensor(
-                out=gained[t][:, cols], in0=acc[:], in1=mixer_gain[:, cols], op=ALU.mult
-            )
 
-        def root_mean_square(sum_of_squares, name):
-            rms = stats.tile([P, 1], F32, name=name)
-            nc.scalar.activation(
-                out=rms[:], in_=sum_of_squares, func=ACT.Sqrt, scale=1.0 / D, bias=eps[:]
+        w_codes = mx.tile([P, PASSES, D], U32, align_bytes=64)
+        w_scales = mx.tile([P, PASSES, D], U8, align_bytes=64)
+        y_codes = mx.tile([P, PASSES, L], U32, align_bytes=64)
+        y_scales = mx.tile([P, PASSES, L], U8, align_bytes=64)
+
+        for c in range(CHUNKS):
+            w_staged = stage.tile([P, PASSES, CHUNK, PACK], BF16, align_bytes=64)
+            rows = slice(c * CHUNK, (c + 1) * CHUNK)
+            quantise_rows(
+                [w_raw[c][:, i, :] for i in range(CHUNK_TILES)],
+                w_staged, w_codes[:, :, rows], w_scales[:, :, rows], c * CHUNK_TILES * TILE_BANKS,
             )
-            return rms
-
-        def inverse(rms, name):
-            inv = stats.tile([P, 1], F32, name=name)
-            nc.vector.reciprocal(out=inv[:], in_=rms[:])
-            return inv
-
         for t in range(L_TILES):
-            quantise_y(t)
-        quantise_w(0)
+            y_staged = stage.tile([P, PASSES, P, PACK], BF16, align_bytes=64)
+            rows = slice(t * P, (t + 1) * P)
+            quantise_rows(
+                [y_raw[t][:]], y_staged, y_codes[:, :, rows], y_scales[:, :, rows],
+                (D // P + t) * TILE_BANKS,
+            )
 
         h = [keep.tile([P, D], F32, name="h%d" % t) for t in range(L_TILES)]
         for t in range(L_TILES):
-            nc.gpsimd.tensor_tensor(out=h[t][:], in0=x_raw[t][:], in1=step_row, op=ALU.add)
+            for c in range(CHUNKS):
+                cols = slice(c * CHUNK, (c + 1) * CHUNK)
+                nc.gpsimd.tensor_tensor(
+                    out=h[t][:, cols], in0=x_raw[t][:, cols], in1=step_row[:, cols], op=ALU.add
+                )
 
-        for c in range(1, CHUNKS):
-            quantise_w(c)
-            for t in range(L_TILES):
-                project(t, c - 1)
-
+        gained = [keep.tile([P, D], F32, name="gained%d" % t) for t in range(L_TILES)]
         v = [keep.tile([P, D], F32, name="v%d" % t) for t in range(L_TILES)]
-        for t in range(L_TILES):
-            project(t, CHUNKS - 1)
-            partial = stats.tile([P, CHUNKS], F32, name="partial%d" % t)
+        p_squares = [stats.tile([P, BANKS], F32, name="p_squares%d" % t) for t in range(L_TILES)]
+
+        def project(t):
+            for n in range(BANKS):
+                cols = slice(n * BANK, (n + 1) * BANK)
+                acc = acc_psum.tile([P, BANK], F32)
+                for g in range(PASSES):
+                    nc.tensor.matmul_mx(
+                        out=acc[:],
+                        lhsT=y_codes[:, g, t * P : (t + 1) * P].bitcast(FP8X4),
+                        lhsT_scale=y_scales[:, g, t * P : (t + 1) * P],
+                        rhs=w_codes[:, g, cols].bitcast(FP8X4),
+                        rhs_scale=w_scales[:, g, cols],
+                        start=(g == 0),
+                        stop=(g == PASSES - 1),
+                    )
+                squares = scrap.tile([P, BANK], BF16, name="squares")
+                nc.scalar.activation(
+                    out=squares[:], in_=acc[:], func=ACT.Square,
+                    accum_out=p_squares[t][:, n : n + 1],
+                )
+                nc.vector.tensor_tensor(
+                    out=gained[t][:, cols], in0=acc[:], in1=mixer_gain[:, cols], op=ALU.mult
+                )
+
+        def inverse_rms(sum_of_squares, name):
+            rms = stats.tile([P, 1], F32, name="rms_" + name)
+            nc.scalar.activation(
+                out=rms[:], in_=sum_of_squares, func=ACT.Sqrt, scale=1.0 / D, bias=eps[:]
+            )
+            inv = stats.tile([P, 1], F32, name="inv_" + name)
+            nc.vector.reciprocal(out=inv[:], in_=rms[:])
+            return inv
+
+        def first_norm(t):
+            partial = stats.tile([P, BANKS], F32, name="partial%d" % t)
             p_square_sum = stats.tile([P, 1], F32, name="p_square_sum%d" % t)
             nc.scalar.activation(
                 out=partial[:], in_=p_squares[t][:], func=ACT.Copy, accum_out=p_square_sum[:]
             )
-            inv_p = inverse(root_mean_square(p_square_sum[:], "rms_p%d" % t), "inv_p%d" % t)
+            inv_p = inverse_rms(p_square_sum[:], "p%d" % t)
             nc.vector.scalar_tensor_tensor(
                 out=v[t][:], in0=gained[t][:], scalar=inv_p[:], in1=h[t][:],
                 op0=ALU.mult, op1=ALU.add,
             )
 
-        for t in range(L_TILES):
+        def second_norm(t):
             v_squares = scrap.tile([P, D], BF16, name="v_squares")
             v_square_sum = stats.tile([P, 1], F32, name="v_square_sum%d" % t)
             nc.scalar.activation(
                 out=v_squares[:], in_=v[t][:], func=ACT.Square, accum_out=v_square_sum[:]
             )
-            inv_v = inverse(root_mean_square(v_square_sum[:], "rms_v%d" % t), "inv_v%d" % t)
+            inv_v = inverse_rms(v_square_sum[:], "v%d" % t)
             result = scrap.tile([P, D], F32, name="result")
-            for n in range(2):
-                cols = slice(n * HALF, (n + 1) * HALF)
+            for n in range(BANKS):
+                cols = slice(n * BANK, (n + 1) * BANK)
                 nc.vector.scalar_tensor_tensor(
                     out=result[:, cols], in0=v[t][:, cols], scalar=inv_v[:], in1=loop_gain[:, cols],
                     op0=ALU.mult, op1=ALU.mult,
                 )
                 nc.sync.dma_start(out=out_rows[t * P : (t + 1) * P, cols], in_=result[:, cols])
+
+        project(0)
+        first_norm(0)
+        for t in range(1, L_TILES):
+            project(t)
+            first_norm(t)
+            second_norm(t - 1)
+        second_norm(L_TILES - 1)

@@ -69,7 +69,7 @@ def tile_recursivemamba130m_pb_kernel(
         eps = consts.tile([P, 1], F32)
         nc.vector.memset(eps[:], EPS)
         warm = consts.tile([P, 1], F32)
-        nc.scalar.activation(out=warm[:], in_=eps[:], func=ACT.Sqrt)
+        nc.scalar.activation(out=warm[:], in_=eps[:], func=ACT.Abs_reciprocal_sqrt)
         ident = consts.tile([P, P], F32)
         make_identity(nc, ident[:])
         ones = consts.tile([P, P], BF16)
@@ -150,6 +150,7 @@ def tile_recursivemamba130m_pb_kernel(
         p_squares = [stats.tile([P, BANKS], F32, name="p_squares%d" % t) for t in range(L_TILES)]
 
         def project(t):
+            folded = eps
             for n in range(BANKS):
                 cols = slice(n * BANK, (n + 1) * BANK)
                 acc = acc_psum.tile([P, BANK], F32)
@@ -171,23 +172,25 @@ def tile_recursivemamba130m_pb_kernel(
                 nc.vector.tensor_tensor(
                     out=gained[t][:, cols], in0=acc[:], in1=mixer_gain[:, cols], op=ALU.mult
                 )
+                if n + 1 < BANKS:
+                    share = stats.tile([P, 1], F32, name="share%d_%d" % (t, n))
+                    nc.scalar.activation(
+                        out=share[:], in_=p_squares[t][:, n : n + 1], func=ACT.Identity,
+                        scale=1.0 / D, bias=folded[:],
+                    )
+                    folded = share
+            return folded
 
-        def inverse_rms(sum_of_squares, name):
-            rms = stats.tile([P, 1], F32, name="rms_" + name)
-            nc.scalar.activation(
-                out=rms[:], in_=sum_of_squares, func=ACT.Sqrt, scale=1.0 / D, bias=eps[:]
-            )
+        def inverse_rms(sum_of_squares, rest, name):
             inv = stats.tile([P, 1], F32, name="inv_" + name)
-            nc.vector.reciprocal(out=inv[:], in_=rms[:])
+            nc.scalar.activation(
+                out=inv[:], in_=sum_of_squares, func=ACT.Abs_reciprocal_sqrt,
+                scale=1.0 / D, bias=rest[:],
+            )
             return inv
 
-        def first_norm(t):
-            partial = stats.tile([P, BANKS], F32, name="partial%d" % t)
-            p_square_sum = stats.tile([P, 1], F32, name="p_square_sum%d" % t)
-            nc.scalar.activation(
-                out=partial[:], in_=p_squares[t][:], func=ACT.Copy, accum_out=p_square_sum[:]
-            )
-            inv_p = inverse_rms(p_square_sum[:], "p%d" % t)
+        def first_norm(t, folded):
+            inv_p = inverse_rms(p_squares[t][:, BANKS - 1 : BANKS], folded, "p%d" % t)
             nc.vector.scalar_tensor_tensor(
                 out=v[t][:], in0=gained[t][:], scalar=inv_p[:], in1=h[t][:],
                 op0=ALU.mult, op1=ALU.add,
@@ -199,7 +202,7 @@ def tile_recursivemamba130m_pb_kernel(
             nc.scalar.activation(
                 out=v_squares[:], in_=v[t][:], func=ACT.Square, accum_out=v_square_sum[:]
             )
-            inv_v = inverse_rms(v_square_sum[:], "v%d" % t)
+            inv_v = inverse_rms(v_square_sum[:], eps, "v%d" % t)
             result = scrap.tile([P, D], F32, name="result")
             for n in range(BANKS):
                 cols = slice(n * BANK, (n + 1) * BANK)
@@ -209,10 +212,8 @@ def tile_recursivemamba130m_pb_kernel(
                 )
                 nc.sync.dma_start(out=out_rows[t * P : (t + 1) * P, cols], in_=result[:, cols])
 
-        project(0)
-        first_norm(0)
+        first_norm(0, project(0))
         for t in range(1, L_TILES):
-            project(t)
-            first_norm(t)
+            first_norm(t, project(t))
             second_norm(t - 1)
         second_norm(L_TILES - 1)

@@ -39,7 +39,6 @@ def tile_recursivemamba130m_pb_kernel(
     out_rows = out.flatten_outer_dims()
 
     with ExitStack() as ctx:
-        ctx.enter_context(tc.manual_schedule())
         consts = ctx.enter_context(tc.tile_pool(name="consts", bufs=1))
         raw = ctx.enter_context(tc.tile_pool(name="raw", bufs=1))
         mx = ctx.enter_context(tc.tile_pool(name="mx", bufs=1))

from contextlib import ExitStack

import concourse.mybir as mybir
from concourse.masks import make_identity

F32 = mybir.dt.float32
BF16 = mybir.dt.bfloat16
I32 = mybir.dt.int32
U32 = mybir.dt.uint32
U8 = mybir.dt.uint8
FP8X4 = mybir.dt.float8_e4m3fn_x4
ACT = mybir.ActivationFunctionType
ALU = mybir.AluOpType

P = 128
L, D, K = 384, 1024, 2048
EPS = 1e-6
PACK = 4
PASSES = K // (P * PACK)
BANK_PASSES = 2
TILE_BANKS = PASSES // BANK_PASSES
L_TILES = L // P
CHUNK = 256
CHUNK_TILES = CHUNK // P
CHUNKS = D // CHUNK
BANK = 512
BANKS = D // BANK
VECTOR_EVERY = 3

FLOPS = 2 * L * D * K


def tile_recursivemamba130m_pb_kernel(
    tc, y, x, step_emb, out_proj_w, mixer_norm_w, loop_norm_w, out
):
    nc = tc.nc
    y_rows = y.flatten_outer_dims()
    x_rows = x.flatten_outer_dims()
    out_rows = out.flatten_outer_dims()

    with ExitStack() as ctx:
        consts = ctx.enter_context(tc.tile_pool(name="consts", bufs=1))
        raw = ctx.enter_context(tc.tile_pool(name="raw", bufs=1))
        mx = ctx.enter_context(tc.tile_pool(name="mx", bufs=1))
        stage = ctx.enter_context(tc.tile_pool(name="stage", bufs=2))
        keep = ctx.enter_context(tc.tile_pool(name="keep", bufs=1))
        scrap = ctx.enter_context(tc.tile_pool(name="scrap", bufs=2))
        stats = ctx.enter_context(tc.tile_pool(name="stats", bufs=1))
        tr_psum = ctx.enter_context(tc.psum_pool(name="tr_psum", bufs=4))
        acc_psum = ctx.enter_context(tc.psum_pool(name="acc_psum", bufs=4))

        vec_in = consts.tile([1, 3, D], BF16)
        for i, vec in enumerate((mixer_norm_w, step_emb, loop_norm_w)):
            nc.sync.dma_start(out=vec_in[:, i, :], in_=vec.unsqueeze(0))
        w_raw = [raw.tile([P, CHUNK_TILES, K], BF16, name="w_raw%d" % c) for c in range(CHUNKS)]
        for c in range(CHUNKS):
            nc.sync.dma_start(
                out=w_raw[c][:],
                in_=out_proj_w[c * CHUNK : (c + 1) * CHUNK, :].rearrange("(i p) k -> p i k", p=P),
            )
        y_raw = [raw.tile([P, K], BF16, name="y_raw%d" % t) for t in range(L_TILES)]
        for t in range(L_TILES):
            nc.sync.dma_start(out=y_raw[t][:], in_=y_rows[t * P : (t + 1) * P, :])
        x_raw = [raw.tile([P, D], BF16, name="x_raw%d" % t) for t in range(L_TILES)]
        for t in range(L_TILES):
            nc.sync.dma_start(out=x_raw[t][:], in_=x_rows[t * P : (t + 1) * P, :])

        eps = consts.tile([P, 1], F32)
        nc.vector.memset(eps[:], EPS)
        warm = consts.tile([P, 1], F32)
        nc.scalar.activation(out=warm[:], in_=eps[:], func=ACT.Abs_reciprocal_sqrt)
        ident = consts.tile([P, P], F32)
        make_identity(nc, ident[:])
        ones = consts.tile([P, P], BF16)
        nc.vector.memset(ones[:], 1.0)

        vec_rows = consts.tile([P, 3, D], BF16)
        nc.vector.memset(vec_rows[:].bitcast(I32), 0)
        nc.vector.tensor_copy(out=vec_rows[0:1, :, :], in_=vec_in[:])
        spread = consts.tile([P, 3, D], BF16)
        for i in range(3):
            bank = tr_psum.tile([P, D], BF16, name="bank")
            for n in range(BANKS):
                cols = slice(n * BANK, (n + 1) * BANK)
                nc.tensor.matmul(
                    out=bank[:, cols], lhsT=ones[:], rhs=vec_rows[:, i, cols], start=True, stop=True
                )
            nc.scalar.copy(out=spread[:, i, :], in_=bank[:])
        mixer_gain = spread[:, 0, :]
        step_row = spread[:, 1, :]
        loop_gain = spread[:, 2, :]

        def quantise_rows(row_tiles, staged, codes, scales, first_bank):
            staged_words = staged[:].bitcast(F32)
            for i, rows in enumerate(row_tiles):
                row_words = rows.bitcast(F32)
                for b in range(TILE_BANKS):
                    bank = tr_psum.tile([P, BANK_PASSES, 2, P], F32, name="bank")
                    for g in range(BANK_PASSES):
                        for u in range(2):
                            first = ((b * BANK_PASSES + g) * 2 + u) * P
                            nc.tensor.transpose(
                                bank[:, g, u, :], row_words[:, first : first + P], ident[:]
                            )
                    passes = slice(b * BANK_PASSES, (b + 1) * BANK_PASSES)
                    dst = staged_words[:, passes, i * P : (i + 1) * P, :]
                    src = bank[:].rearrange("p g u r -> p g r u")
                    if (first_bank + i * TILE_BANKS + b) % VECTOR_EVERY == 0:
                        nc.vector.tensor_copy(out=dst, in_=src)
                    else:
                        nc.scalar.copy(out=dst, in_=src)
            for g in range(PASSES):
                nc.vector.quantize_mx(
                    out=codes[:, g, :].bitcast(FP8X4),
                    scales=scales[:, g, :],
                    in_=staged[:, g, :, :].rearrange("p r t -> p (r t)"),
                )

        w_codes = mx.tile([P, PASSES, D], U32, align_bytes=64)
        w_scales = mx.tile([P, PASSES, D], U8, align_bytes=64)
        y_codes = mx.tile([P, PASSES, L], U32, align_bytes=64)
        y_scales = mx.tile([P, PASSES, L], U8, align_bytes=64)

        for c in range(CHUNKS):
            w_staged = stage.tile([P, PASSES, CHUNK, PACK], BF16, align_bytes=64)
            rows = slice(c * CHUNK, (c + 1) * CHUNK)
            quantise_rows(
                [w_raw[c][:, i, :] for i in range(CHUNK_TILES)],
                w_staged, w_codes[:, :, rows], w_scales[:, :, rows], c * CHUNK_TILES * TILE_BANKS,
            )
        for t in range(L_TILES):
            y_staged = stage.tile([P, PASSES, P, PACK], BF16, align_bytes=64)
            rows = slice(t * P, (t + 1) * P)
            quantise_rows(
                [y_raw[t][:]], y_staged, y_codes[:, :, rows], y_scales[:, :, rows],
                (D // P + t) * TILE_BANKS,
            )

        h = [keep.tile([P, D], F32, name="h%d" % t) for t in range(L_TILES)]
        for t in range(L_TILES):
            for c in range(CHUNKS):
                cols = slice(c * CHUNK, (c + 1) * CHUNK)
                nc.gpsimd.tensor_tensor(
                    out=h[t][:, cols], in0=x_raw[t][:, cols], in1=step_row[:, cols], op=ALU.add
                )

        gained = [keep.tile([P, D], F32, name="gained%d" % t) for t in range(L_TILES)]
        v = [keep.tile([P, D], F32, name="v%d" % t) for t in range(L_TILES)]
        p_squares = [stats.tile([P, BANKS], F32, name="p_squares%d" % t) for t in range(L_TILES)]

        def project(t):
            folded = eps
            for n in range(BANKS):
                cols = slice(n * BANK, (n + 1) * BANK)
                acc = acc_psum.tile([P, BANK], F32)
                for g in range(PASSES):
                    nc.tensor.matmul_mx(
                        out=acc[:],
                        lhsT=y_codes[:, g, t * P : (t + 1) * P].bitcast(FP8X4),
                        lhsT_scale=y_scales[:, g, t * P : (t + 1) * P],
                        rhs=w_codes[:, g, cols].bitcast(FP8X4),
                        rhs_scale=w_scales[:, g, cols],
                        start=(g == 0),
                        stop=(g == PASSES - 1),
                    )
                squares = scrap.tile([P, BANK], BF16, name="squares")
                nc.scalar.activation(
                    out=squares[:], in_=acc[:], func=ACT.Square,
                    accum_out=p_squares[t][:, n : n + 1],
                )
                nc.vector.tensor_tensor(
                    out=gained[t][:, cols], in0=acc[:], in1=mixer_gain[:, cols], op=ALU.mult
                )
                if n + 1 < BANKS:
                    share = stats.tile([P, 1], F32, name="share%d_%d" % (t, n))
                    nc.scalar.activation(
                        out=share[:], in_=p_squares[t][:, n : n + 1], func=ACT.Identity,
                        scale=1.0 / D, bias=folded[:],
                    )
                    folded = share
            return folded

        def inverse_rms(sum_of_squares, rest, name):
            inv = stats.tile([P, 1], F32, name="inv_" + name)
            nc.scalar.activation(
                out=inv[:], in_=sum_of_squares, func=ACT.Abs_reciprocal_sqrt,
                scale=1.0 / D, bias=rest[:],
            )
            return inv

        def first_norm(t, folded):
            inv_p = inverse_rms(p_squares[t][:, BANKS - 1 : BANKS], folded, "p%d" % t)
            nc.vector.scalar_tensor_tensor(
                out=v[t][:], in0=gained[t][:], scalar=inv_p[:], in1=h[t][:],
                op0=ALU.mult, op1=ALU.add,
            )

        def second_norm(t):
            v_squares = scrap.tile([P, D], BF16, name="v_squares")
            v_square_sum = stats.tile([P, 1], F32, name="v_square_sum%d" % t)
            nc.scalar.activation(
                out=v_squares[:], in_=v[t][:], func=ACT.Square, accum_out=v_square_sum[:]
            )
            inv_v = inverse_rms(v_square_sum[:], eps, "v%d" % t)
            result = scrap.tile([P, D], F32, name="result")
            for n in range(BANKS):
                cols = slice(n * BANK, (n + 1) * BANK)
                nc.vector.scalar_tensor_tensor(
                    out=result[:, cols], in0=v[t][:, cols], scalar=inv_v[:], in1=loop_gain[:, cols],
                    op0=ALU.mult, op1=ALU.mult,
                )
                nc.sync.dma_start(out=out_rows[t * P : (t + 1) * P, cols], in_=result[:, cols])

        first_norm(0, project(0))
        for t in range(1, L_TILES):
            first_norm(t, project(t))
            second_norm(t - 1)
        second_norm(L_TILES - 1)
